import numpy as np
import ml_dtypes


def mxq(x, axis, fmt="e4m3"):
    dtype, down = {"e4m3": (ml_dtypes.float8_e4m3fn, 7), "e5m2": (ml_dtypes.float8_e5m2, 14)}[fmt]
    v = np.moveaxis(np.asarray(x, np.float32).astype(ml_dtypes.bfloat16).astype(np.float64), axis, -1)
    blocks = v.reshape(v.shape[:-1] + (-1, 32))
    amax = np.abs(blocks).max(-1, keepdims=True)
    byte = np.maximum(np.where(amax > 0, np.frexp(amax)[1] - 1 + 127, 0) - down, 1)
    scale = np.exp2(byte - 127.0)
    codes = (blocks / scale).astype(np.float32).astype(dtype).astype(np.float64)
    return np.moveaxis((codes * scale).reshape(v.shape), -1, axis)


WIDE = False


def mx_kscale(k):
    if not WIDE:
        return np.ones(k)
    levels = np.array([10, -10, 5, -5, 0])
    a = np.random.permutation(np.resize(levels, k // 512 * 4)).reshape(k // 512, 4)
    idx = np.arange(k)
    return np.exp2(a[idx // 512, idx % 128 // 32])


BF16 = ml_dtypes.bfloat16


def bf(x):
    return np.asarray(x, np.float32).astype(BF16)


def f64(x):
    return np.asarray(x).astype(np.float64)


E2M1 = np.array([0.0, 0.5, 1.0, 1.5, 2.0, 3.0, 4.0, 6.0, -0.0, -0.5, -1.0, -1.5, -2.0, -3.0, -4.0, -6.0])


def pack_weight(w, fmt):
    k, n = w.shape
    w = f64(bf(w)).reshape(k // 32, 32, n)
    amax = np.abs(w).max(1)
    if fmt == "e4m3":
        byte = np.frexp(amax)[1] - 1 + 127 - 7
    else:
        mant, ex = np.frexp(amax / 6.0)
        byte = np.where(mant > 0.5, ex, ex - 1) + 127
    byte = np.clip(np.where(amax > 0, byte, 1), 1, 254)
    scaled = (w * np.exp2(127.0 - byte)[:, None, :]).reshape(k, n).astype(np.float32)
    by_word = np.ascontiguousarray(scaled.reshape(k // 512, 128, 4, n).transpose(0, 1, 3, 2))
    if fmt == "e4m3":
        words = by_word.astype(ml_dtypes.float8_e4m3fn).view(np.uint8)
    else:
        c = by_word.astype(ml_dtypes.float4_e2m1fn).view(np.uint8) & 0xF
        words = c[..., 0::2] | (c[..., 1::2] << 4)
    return np.ascontiguousarray(words), np.ascontiguousarray(byte.astype(np.uint8).reshape(k // 512, 16, n))


def unpack_weight(words, scales, fmt):
    g, p, n, _ = words.shape
    if fmt == "e4m3":
        vals = np.ascontiguousarray(words).view(ml_dtypes.float8_e4m3fn).astype(np.float64)
    else:
        nib = np.empty((g, p, n, 4), np.uint8)
        nib[..., 0::2] = words & 0xF
        nib[..., 1::2] = words >> 4
        vals = E2M1[nib]
    vals = vals * np.repeat(np.exp2(scales.astype(np.float64) - 127.0), 8, axis=1)[..., None]
    return vals.transpose(0, 1, 3, 2).reshape(g * 512, n)


B, IN, H = 128, 1024, 2048
MX_PASS = 512
QH = H % MX_PASS == 0
FMT = "e4m3"


def sigmoid(v):
    return 1.0 / (1.0 + np.exp(-v))


def setup_inputs():
    s = mx_kscale(IN)
    t = mx_kscale(H) if QH else np.ones(H)
    inp = {"x": bf(np.random.standard_normal((B, IN)) * s),
           "h0": bf(np.random.standard_normal((B, H)) * t),
           "c0": bf(np.random.standard_normal((B, H)))}
    for name in ("xi", "xf", "xo", "xc"):
        w = np.random.uniform(-1.0, 1.0, (H, IN)) / np.sqrt(IN) / s
        words, scales = pack_weight(np.ascontiguousarray(w.T), FMT)
        inp["W_" + name + "_words"] = words
        inp["W_" + name + "_scales"] = scales
    for name in ("xi", "xf", "xo", "xc"):
        inp["b_" + name] = bf(np.random.standard_normal(H) * 0.3)
    for name in ("hi", "hf", "ho", "hc"):
        w = np.random.uniform(-1.0, 1.0, (H, H)) / np.sqrt(H) / t
        words, scales = pack_weight(np.ascontiguousarray(w.T), FMT)
        inp["W_" + name + "_words"] = words
        inp["W_" + name + "_scales"] = scales
    return inp


def reference(x, h0, c0,
              W_xi_words, W_xi_scales, W_xf_words, W_xf_scales,
              W_xo_words, W_xo_scales, W_xc_words, W_xc_scales,
              b_xi, b_xf, b_xo, b_xc,
              W_hi_words, W_hi_scales, W_hf_words, W_hf_scales,
              W_ho_words, W_ho_scales, W_hc_words, W_hc_scales):
    Wx = np.concatenate([unpack_weight(W_xi_words, W_xi_scales, FMT),
                         unpack_weight(W_xf_words, W_xf_scales, FMT),
                         unpack_weight(W_xo_words, W_xo_scales, FMT),
                         unpack_weight(W_xc_words, W_xc_scales, FMT)], axis=1).T
    bx = np.concatenate([f64(b_xi), f64(b_xf), f64(b_xo), f64(b_xc)], axis=0)
    Wh = np.concatenate([unpack_weight(W_hi_words, W_hi_scales, FMT),
                         unpack_weight(W_hf_words, W_hf_scales, FMT),
                         unpack_weight(W_ho_words, W_ho_scales, FMT),
                         unpack_weight(W_hc_words, W_hc_scales, FMT)], axis=1).T
    gx = mxq(f64(x), 1, "e4m3") @ Wx.T
    if QH:
        gh = mxq(f64(h0), 1, "e4m3") @ Wh.T
    else:
        gh = f64(h0) @ Wh.T
    g = gx + bx + gh
    gi, gf, go, gc = np.split(g, 4, axis=1)
    i_t = sigmoid(gi)
    f_t = sigmoid(gf)
    o_t = sigmoid(go)
    c_tilde = np.tanh(gc)
    c_t = f_t * f64(c0) + i_t * c_tilde
    h_t = o_t * np.tanh(c_t)
    return (h_t, c_t)

@@ -1,0 +1,182 @@
+from contextlib import ExitStack
+
+import concourse.mybir as mybir
+from concourse.masks import make_identity
+
+F32 = mybir.dt.float32
+BF16 = mybir.dt.bfloat16
+I32 = mybir.dt.int32
+U32 = mybir.dt.uint32
+U8 = mybir.dt.uint8
+FP8X4 = mybir.dt.float8_e4m3fn_x4
+ACT = mybir.ActivationFunctionType
+ALU = mybir.AluOpType
+
+P = 128
+B, IN, H = 128, 1024, 2048
+NB = 512
+NJ = H // NB
+FLOPS = 2 * B * (IN + H) * 4 * H
+
+W_BUFS = 14
+SCALE_QUEUE = ("sync", "sync", "sync", "sync")
+LAST_SPLIT = 4
+
+
+def tile_simplelstm_w_kernel(
+    tc, x, h0, c0,
+    W_xi_words, W_xi_scales, W_xf_words, W_xf_scales,
+    W_xo_words, W_xo_scales, W_xc_words, W_xc_scales,
+    b_xi, b_xf, b_xo, b_xc,
+    W_hi_words, W_hi_scales, W_hf_words, W_hf_scales,
+    W_ho_words, W_ho_scales, W_hc_words, W_hc_scales,
+    out_0, out_1,
+):
+    nc = tc.nc
+    gates = (
+        ("i", W_xi_words, W_xi_scales, W_hi_words, W_hi_scales, b_xi, ACT.Sigmoid),
+        ("c", W_xc_words, W_xc_scales, W_hc_words, W_hc_scales, b_xc, ACT.Tanh),
+        ("f", W_xf_words, W_xf_scales, W_hf_words, W_hf_scales, b_xf, ACT.Sigmoid),
+        ("o", W_xo_words, W_xo_scales, W_ho_words, W_ho_scales, b_xo, ACT.Sigmoid),
+    )
+    with ExitStack() as ctx:
+        keep = ctx.enter_context(tc.tile_pool(name="keep", bufs=1))
+        wpool = ctx.enter_context(tc.tile_pool(name="weights", bufs=W_BUFS))
+        accp = ctx.enter_context(tc.psum_pool(name="acc", bufs=6))
+        auxp = ctx.enter_context(tc.psum_pool(name="aux", bufs=2))
+
+        x_sb = keep.tile([P, IN], BF16, name="x_sb")
+        nc.sync.dma_start(out=x_sb[:], in_=x)
+        h_sb = keep.tile([P, H], BF16, name="h_sb")
+        nc.sync.dma_start(out=h_sb[:], in_=h0)
+        c_sb = keep.tile([P, H], BF16, name="c_sb")
+        nc.sync.dma_start(out=c_sb[:], in_=c0)
+
+        xplanes = [keep.tile([P, H], U8, name="xplane%d" % s, align_bytes=64) for s in range(2)]
+        hplanes = [keep.tile([P, H], U8, name="hplane%d" % q, align_bytes=64) for q in range(4)]
+        for q in range(4):
+            if q % 2 == 0:
+                nc.vector.memset(xplanes[q // 2][:].bitcast(I32), 0)
+            nc.vector.memset(hplanes[q][:].bitcast(I32), 0)
+
+        ident = keep.tile([P, P], F32, name="ident")
+        make_identity(nc, ident[:])
+        brow = keep.tile([P, H], BF16, name="brow")
+        nc.vector.memset(brow[:].bitcast(I32), 0)
+        sel = keep.tile([P, 4, P], BF16, name="sel")
+        nc.vector.memset(sel[:], 0.0)
+        for q in range(4):
+            nc.vector.memset(sel[32 * q:32 * q + 1, q, :], 1.0)
+
+        for q in range(4):
+            nc.scalar.dma_start(out=brow[32 * q:32 * q + 1, :], in_=gates[q][5].rearrange("(o n) -> o n", o=1))
+
+        def load_scales(q):
+            sx, sh = gates[q][2], gates[q][4]
+            xp, hp = xplanes[q // 2], hplanes[q]
+            lo = 8 * (q % 2)
+            for quad in range(4):
+                dst = xp[32 * quad + lo:32 * quad + lo + 8, :]
+                src = sx[:, 4 * quad:4 * quad + 4, :]
+                if SCALE_QUEUE[q] == "sync":
+                    nc.sync.dma_start(out=dst.bitcast(I32), in_=src.bitcast(I32))
+                else:
+                    nc.gpsimd.dma_start(out=dst.bitcast(F32), in_=src.bitcast(F32))
+            for quad in range(4):
+                dst = hp[32 * quad:32 * quad + 16, :]
+                src = sh[:, 4 * quad:4 * quad + 4, :]
+                if SCALE_QUEUE[q] == "sync":
+                    nc.sync.dma_start(out=dst.bitcast(I32), in_=src.bitcast(I32))
+                else:
+                    nc.gpsimd.dma_start(out=dst.bitcast(F32), in_=src.bitcast(F32))
+
+        for q in range(4):
+            if SCALE_QUEUE[q] != "sync":
+                load_scales(q)
+
+        a_codes = keep.tile([P, 6 * P], U32, name="a_codes", align_bytes=64)
+        a_scales = keep.tile([P, 6 * P], U8, name="a_scales", align_bytes=64)
+        sources = (
+            x_sb[:].bitcast(F32),
+            h_sb[:].bitcast(F32)[:, 0:512],
+            h_sb[:].bitcast(F32)[:, 512:1024],
+        )
+        grouped = []
+        for s, words in enumerate(sources):
+            bank = auxp.tile([P, 4, P], F32, name="tp", tag="aux")
+            for g in range(2):
+                for u in range(2):
+                    nc.tensor.transpose(
+                        bank[:, 2 * g + u, :],
+                        words[:, 256 * g + u:256 * (g + 1):2],
+                        ident[:],
+                    )
+            grp = keep.tile([P, 1024], BF16, name="grouped%d" % s, align_bytes=64)
+            nc.vector.tensor_copy(
+                out=grp[:].bitcast(F32).rearrange("p (g m u) -> p g m u", g=2, u=2),
+                in_=bank[:].rearrange("p (g u) m -> p g m u", u=2),
+            )
+            grouped.append(grp)
+        for s in range(3):
+            nc.vector.quantize_mx(
+                out=a_codes[:, 256 * s:256 * (s + 1)].bitcast(FP8X4),
+                scales=a_scales[:, 256 * s:256 * (s + 1)],
+                in_=grouped[s][:],
+            )
+
+        bias_bc = keep.tile([P, 4, H], BF16, name="bias_bc")
+        z = {}
+        c_t = keep.tile([P, H], F32, name="c_t")
+        tanh_c = keep.tile([P, H], F32, name="tanh_c")
+
+        for q, (name, wx, sx, wh, sh, bias, func) in enumerate(gates):
+            if SCALE_QUEUE[q] == "sync":
+                load_scales(q)
+
+            chunks = [(wx, g, g, xplanes[q // 2], 8 * (q % 2) + 4 * g) for g in range(2)]
+            chunks += [(wh, g, 2 + g, hplanes[q], 4 * g) for g in range(4)]
+            acc = [accp.tile([P, NB], F32, name="acc%d" % j, tag="acc") for j in range(NJ)]
+            for ci, (w, g, a, plane, k) in enumerate(chunks):
+                wt = wpool.tile([P, H], U32, name="wt", tag="wt", align_bytes=64)
+                pieces = LAST_SPLIT if (q == 3 and ci == 5) else 1
+                wid = H // pieces
+                for s in range(pieces):
+                    nc.sync.dma_start(
+                        out=wt[:, wid * s:wid * (s + 1)].bitcast(I32),
+                        in_=w[g, :, wid * s:wid * (s + 1), :].rearrange("p n t -> p (n t)").bitcast(I32),
+                    )
+                for j in range(NJ):
+                    js = slice(NB * j, NB * (j + 1))
+                    nc.tensor.matmul_mx(
+                        out=acc[j][:],
+                        lhsT=a_codes[:, P * a:P * (a + 1)].bitcast(FP8X4),
+                        lhsT_scale=a_scales[:, P * a:P * (a + 1)],
+                        rhs=wt[:, js].bitcast(FP8X4),
+                        rhs_scale=plane[k:P, js],
+                        start=(ci == 0),
+                        stop=(ci == 5),
+                    )
+                if ci == 1:
+                    for j in range(NJ):
+                        js = slice(NB * j, NB * (j + 1))
+                        pb = auxp.tile([P, NB], F32, name="pb", tag="aux")
+                        nc.tensor.matmul(out=pb[:], lhsT=sel[:, q, :], rhs=brow[:, js], start=True, stop=True)
+                        nc.scalar.copy(out=bias_bc[:, q, js], in_=pb[:])
+
+            zq = keep.tile([P, H], F32, name="z_" + name)
+            z[name] = zq
+            for j in range(NJ):
+                js = slice(NB * j, NB * (j + 1))
+                nc.vector.tensor_tensor(out=zq[:, js], in0=acc[j][:], in1=bias_bc[:, q, js], op=ALU.add)
+                nc.scalar.activation(out=zq[:, js], in_=zq[:, js], func=func)
+                if name == "c":
+                    nc.vector.tensor_tensor(out=zq[:, js], in0=zq[:, js], in1=z["i"][:, js], op=ALU.mult)
+                if name == "f":
+                    nc.vector.tensor_tensor(out=zq[:, js], in0=zq[:, js], in1=c_sb[:, js], op=ALU.mult)
+                    nc.vector.tensor_tensor(out=c_t[:, js], in0=zq[:, js], in1=z["c"][:, js], op=ALU.add)
+                    nc.scalar.activation(out=tanh_c[:, js], in_=c_t[:, js], func=ACT.Tanh)
+                if name == "o":
+                    nc.vector.tensor_tensor(out=zq[:, js], in0=zq[:, js], in1=tanh_c[:, js], op=ALU.mult)
+                    nc.sync.dma_start(out=out_0[:, js], in_=zq[:, js])
+            if name == "f":
+                nc.scalar.dma_start(out=out_1, in_=c_t[:])

@@ -19,7 +19,7 @@ NJ = H // NB
 FLOPS = 2 * B * (IN + H) * 4 * H
 
 W_BUFS = 14
-SCALE_QUEUE = ("sync", "sync", "sync", "sync")
+SCALE_QUEUE = ("gpsimd", "gpsimd", "gpsimd", "gpsimd")
 LAST_SPLIT = 4
 
 

@@ -19,8 +19,7 @@ NJ = H // NB
 FLOPS = 2 * B * (IN + H) * 4 * H
 
 W_BUFS = 14
-SCALE_QUEUE = ("gpsimd", "gpsimd", "gpsimd", "gpsimd")
-LAST_SPLIT = 4
+TAPER = 2
 
 
 def tile_simplelstm_w_kernel(
@@ -39,6 +38,7 @@ def tile_simplelstm_w_kernel(
         ("f", W_xf_words, W_xf_scales, W_hf_words, W_hf_scales, b_xf, ACT.Sigmoid),
         ("o", W_xo_words, W_xo_scales, W_ho_words, W_ho_scales, b_xo, ACT.Sigmoid),
     )
+    cols = [slice(NB * j, NB * (j + 1)) for j in range(NJ)]
     with ExitStack() as ctx:
         keep = ctx.enter_context(tc.tile_pool(name="keep", bufs=1))
         wpool = ctx.enter_context(tc.tile_pool(name="weights", bufs=W_BUFS))
@@ -67,32 +67,22 @@ def tile_simplelstm_w_kernel(
         nc.vector.memset(sel[:], 0.0)
         for q in range(4):
             nc.vector.memset(sel[32 * q:32 * q + 1, q, :], 1.0)
-
         for q in range(4):
             nc.scalar.dma_start(out=brow[32 * q:32 * q + 1, :], in_=gates[q][5].rearrange("(o n) -> o n", o=1))
 
-        def load_scales(q):
+        for q in range(4):
             sx, sh = gates[q][2], gates[q][4]
-            xp, hp = xplanes[q // 2], hplanes[q]
             lo = 8 * (q % 2)
             for quad in range(4):
-                dst = xp[32 * quad + lo:32 * quad + lo + 8, :]
-                src = sx[:, 4 * quad:4 * quad + 4, :]
-                if SCALE_QUEUE[q] == "sync":
-                    nc.sync.dma_start(out=dst.bitcast(I32), in_=src.bitcast(I32))
-                else:
-                    nc.gpsimd.dma_start(out=dst.bitcast(F32), in_=src.bitcast(F32))
+                nc.gpsimd.dma_start(
+                    out=xplanes[q // 2][32 * quad + lo:32 * quad + lo + 8, :].bitcast(F32),
+                    in_=sx[:, 4 * quad:4 * quad + 4, :].bitcast(F32),
+                )
             for quad in range(4):
-                dst = hp[32 * quad:32 * quad + 16, :]
-                src = sh[:, 4 * quad:4 * quad + 4, :]
-                if SCALE_QUEUE[q] == "sync":
-                    nc.sync.dma_start(out=dst.bitcast(I32), in_=src.bitcast(I32))
-                else:
-                    nc.gpsimd.dma_start(out=dst.bitcast(F32), in_=src.bitcast(F32))
-
-        for q in range(4):
-            if SCALE_QUEUE[q] != "sync":
-                load_scales(q)
+                nc.gpsimd.dma_start(
+                    out=hplanes[q][32 * quad:32 * quad + 16, :].bitcast(F32),
+                    in_=sh[:, 4 * quad:4 * quad + 4, :].bitcast(F32),
+                )
 
         a_codes = keep.tile([P, 6 * P], U32, name="a_codes", align_bytes=64)
         a_scales = keep.tile([P, 6 * P], U8, name="a_scales", align_bytes=64)
@@ -129,46 +119,40 @@ def tile_simplelstm_w_kernel(
         c_t = keep.tile([P, H], F32, name="c_t")
         tanh_c = keep.tile([P, H], F32, name="tanh_c")
 
-        for q, (name, wx, sx, wh, sh, bias, func) in enumerate(gates):
-            if SCALE_QUEUE[q] == "sync":
-                load_scales(q)
+        def load(wt, w, g, js):
+            nc.sync.dma_start(
+                out=wt[:, js].bitcast(I32),
+                in_=w[g, :, js, :].rearrange("p n t -> p (n t)").bitcast(I32),
+            )
 
+        for q, (name, wx, sx, wh, sh, bias, func) in enumerate(gates):
             chunks = [(wx, g, g, xplanes[q // 2], 8 * (q % 2) + 4 * g) for g in range(2)]
             chunks += [(wh, g, 2 + g, hplanes[q], 4 * g) for g in range(4)]
+            last = len(chunks) - 1
+            whole = len(chunks) - (TAPER if q == 3 else 0)
             acc = [accp.tile([P, NB], F32, name="acc%d" % j, tag="acc") for j in range(NJ)]
-            for ci, (w, g, a, plane, k) in enumerate(chunks):
-                wt = wpool.tile([P, H], U32, name="wt", tag="wt", align_bytes=64)
-                pieces = LAST_SPLIT if (q == 3 and ci == 5) else 1
-                wid = H // pieces
-                for s in range(pieces):
-                    nc.sync.dma_start(
-                        out=wt[:, wid * s:wid * (s + 1)].bitcast(I32),
-                        in_=w[g, :, wid * s:wid * (s + 1), :].rearrange("p n t -> p (n t)").bitcast(I32),
-                    )
-                for j in range(NJ):
-                    js = slice(NB * j, NB * (j + 1))
-                    nc.tensor.matmul_mx(
-                        out=acc[j][:],
-                        lhsT=a_codes[:, P * a:P * (a + 1)].bitcast(FP8X4),
-                        lhsT_scale=a_scales[:, P * a:P * (a + 1)],
-                        rhs=wt[:, js].bitcast(FP8X4),
-                        rhs_scale=plane[k:P, js],
-                        start=(ci == 0),
-                        stop=(ci == 5),
-                    )
-                if ci == 1:
-                    for j in range(NJ):
-                        js = slice(NB * j, NB * (j + 1))
-                        pb = auxp.tile([P, NB], F32, name="pb", tag="aux")
-                        nc.tensor.matmul(out=pb[:], lhsT=sel[:, q, :], rhs=brow[:, js], start=True, stop=True)
-                        nc.scalar.copy(out=bias_bc[:, q, js], in_=pb[:])
-
             zq = keep.tile([P, H], F32, name="z_" + name)
             z[name] = zq
-            for j in range(NJ):
-                js = slice(NB * j, NB * (j + 1))
+
+            def mx_pass(ci, wt, j):
+                a, plane, k = chunks[ci][2], chunks[ci][3], chunks[ci][4]
+                nc.tensor.matmul_mx(
+                    out=acc[j][:],
+                    lhsT=a_codes[:, P * a:P * (a + 1)].bitcast(FP8X4),
+                    lhsT_scale=a_scales[:, P * a:P * (a + 1)],
+                    rhs=wt[:, cols[j]].bitcast(FP8X4),
+                    rhs_scale=plane[k:P, cols[j]],
+                    start=(ci == 0),
+                    stop=(ci == last),
+                )
+
+            def gate_value(j):
+                js = cols[j]
                 nc.vector.tensor_tensor(out=zq[:, js], in0=acc[j][:], in1=bias_bc[:, q, js], op=ALU.add)
                 nc.scalar.activation(out=zq[:, js], in_=zq[:, js], func=func)
+
+            def combine(j):
+                js = cols[j]
                 if name == "c":
                     nc.vector.tensor_tensor(out=zq[:, js], in0=zq[:, js], in1=z["i"][:, js], op=ALU.mult)
                 if name == "f":
@@ -178,5 +162,29 @@ def tile_simplelstm_w_kernel(
                 if name == "o":
                     nc.vector.tensor_tensor(out=zq[:, js], in0=zq[:, js], in1=tanh_c[:, js], op=ALU.mult)
                     nc.sync.dma_start(out=out_0[:, js], in_=zq[:, js])
-            if name == "f":
-                nc.scalar.dma_start(out=out_1, in_=c_t[:])
+
+            for ci in range(whole):
+                wt = wpool.tile([P, H], U32, name="wt", tag="wt", align_bytes=64)
+                load(wt, chunks[ci][0], chunks[ci][1], slice(0, H))
+                for j in range(NJ):
+                    mx_pass(ci, wt, j)
+                if ci == 1:
+                    for j in range(NJ):
+                        pb = auxp.tile([P, NB], F32, name="pb", tag="aux")
+                        nc.tensor.matmul(out=pb[:], lhsT=sel[:, q, :], rhs=brow[:, cols[j]], start=True, stop=True)
+                        nc.scalar.copy(out=bias_bc[:, q, cols[j]], in_=pb[:])
+
+            tapered = [wpool.tile([P, H], U32, name="wt", tag="wt", align_bytes=64) for ci in range(whole, len(chunks))]
+            for j in range(NJ):
+                for ci in range(whole, len(chunks)):
+                    load(tapered[ci - whole], chunks[ci][0], chunks[ci][1], cols[j])
+            if q == 3:
+                nc.sync.dma_start(out=out_1, in_=c_t[:])
+
+            for j in range(NJ):
+                for ci in range(whole, len(chunks)):
+                    mx_pass(ci, tapered[ci - whole], j)
+                gate_value(j)
+                if j > 0:
+                    combine(j - 1)
+            combine(NJ - 1)

@@ -44,6 +44,7 @@ def tile_simplelstm_w_kernel(
         wpool = ctx.enter_context(tc.tile_pool(name="weights", bufs=W_BUFS))
         accp = ctx.enter_context(tc.psum_pool(name="acc", bufs=6))
         auxp = ctx.enter_context(tc.psum_pool(name="aux", bufs=2))
+        ctx.enter_context(tc.manual_schedule())
 
         x_sb = keep.tile([P, IN], BF16, name="x_sb")
         nc.sync.dma_start(out=x_sb[:], in_=x)

@@ -116,6 +116,14 @@ def tile_simplelstm_w_kernel(
             )
 
         bias_bc = keep.tile([P, 4, H], BF16, name="bias_bc")
+        for q in range(4):
+            for j in range(NJ):
+                pb = auxp.tile([P, NB], F32, name="pb", tag="aux")
+                nc.tensor.matmul(out=pb[:], lhsT=sel[:, q, :], rhs=brow[:, cols[j]], start=True, stop=True)
+                if j % 2 == 0:
+                    nc.scalar.copy(out=bias_bc[:, q, cols[j]], in_=pb[:])
+                else:
+                    nc.vector.tensor_copy(out=bias_bc[:, q, cols[j]], in_=pb[:])
         z = {}
         c_t = keep.tile([P, H], F32, name="c_t")
         tanh_c = keep.tile([P, H], F32, name="tanh_c")
@@ -169,11 +177,6 @@ def tile_simplelstm_w_kernel(
                 load(wt, chunks[ci][0], chunks[ci][1], slice(0, H))
                 for j in range(NJ):
                     mx_pass(ci, wt, j)
-                if ci == 1:
-                    for j in range(NJ):
-                        pb = auxp.tile([P, NB], F32, name="pb", tag="aux")
-                        nc.tensor.matmul(out=pb[:], lhsT=sel[:, q, :], rhs=brow[:, cols[j]], start=True, stop=True)
-                        nc.scalar.copy(out=bias_bc[:, q, cols[j]], in_=pb[:])
 
             tapered = [wpool.tile([P, H], U32, name="wt", tag="wt", align_bytes=64) for ci in range(whole, len(chunks))]
             for j in range(NJ):

@@ -16,10 +16,10 @@ P = 128
 B, IN, H = 128, 1024, 2048
 NB = 512
 NJ = H // NB
+PAIRS = 3
 FLOPS = 2 * B * (IN + H) * 4 * H
 
-W_BUFS = 14
-TAPER = 2
+W_BUFS = 7
 
 
 def tile_simplelstm_w_kernel(
@@ -44,7 +44,6 @@ def tile_simplelstm_w_kernel(
         wpool = ctx.enter_context(tc.tile_pool(name="weights", bufs=W_BUFS))
         accp = ctx.enter_context(tc.psum_pool(name="acc", bufs=6))
         auxp = ctx.enter_context(tc.psum_pool(name="aux", bufs=2))
-        ctx.enter_context(tc.manual_schedule())
 
         x_sb = keep.tile([P, IN], BF16, name="x_sb")
         nc.sync.dma_start(out=x_sb[:], in_=x)
@@ -85,8 +84,8 @@ def tile_simplelstm_w_kernel(
                     in_=sh[:, 4 * quad:4 * quad + 4, :].bitcast(F32),
                 )
 
-        a_codes = keep.tile([P, 6 * P], U32, name="a_codes", align_bytes=64)
-        a_scales = keep.tile([P, 6 * P], U8, name="a_scales", align_bytes=64)
+        a_codes = keep.tile([P, PAIRS, 2, P], U32, name="a_codes", align_bytes=64)
+        a_scales = keep.tile([P, PAIRS, 2, P], U8, name="a_scales", align_bytes=64)
         sources = (
             x_sb[:].bitcast(F32),
             h_sb[:].bitcast(F32)[:, 0:512],
@@ -108,51 +107,43 @@ def tile_simplelstm_w_kernel(
                 in_=bank[:].rearrange("p (g u) m -> p g m u", u=2),
             )
             grouped.append(grp)
-        for s in range(3):
+        for s in range(PAIRS):
             nc.vector.quantize_mx(
-                out=a_codes[:, 256 * s:256 * (s + 1)].bitcast(FP8X4),
-                scales=a_scales[:, 256 * s:256 * (s + 1)],
+                out=a_codes[:, s, :, :].rearrange("p g m -> p (g m)").bitcast(FP8X4),
+                scales=a_scales[:, s, :, :].rearrange("p g m -> p (g m)"),
                 in_=grouped[s][:],
             )
 
         bias_bc = keep.tile([P, 4, H], BF16, name="bias_bc")
-        for q in range(4):
-            for j in range(NJ):
-                pb = auxp.tile([P, NB], F32, name="pb", tag="aux")
-                nc.tensor.matmul(out=pb[:], lhsT=sel[:, q, :], rhs=brow[:, cols[j]], start=True, stop=True)
-                if j % 2 == 0:
-                    nc.scalar.copy(out=bias_bc[:, q, cols[j]], in_=pb[:])
-                else:
-                    nc.vector.tensor_copy(out=bias_bc[:, q, cols[j]], in_=pb[:])
         z = {}
         c_t = keep.tile([P, H], F32, name="c_t")
         tanh_c = keep.tile([P, H], F32, name="tanh_c")
 
-        def load(wt, w, g, js):
-            nc.sync.dma_start(
-                out=wt[:, js].bitcast(I32),
-                in_=w[g, :, js, :].rearrange("p n t -> p (n t)").bitcast(I32),
-            )
-
         for q, (name, wx, sx, wh, sh, bias, func) in enumerate(gates):
-            chunks = [(wx, g, g, xplanes[q // 2], 8 * (q % 2) + 4 * g) for g in range(2)]
-            chunks += [(wh, g, 2 + g, hplanes[q], 4 * g) for g in range(4)]
-            last = len(chunks) - 1
-            whole = len(chunks) - (TAPER if q == 3 else 0)
+            final_gate = q == len(gates) - 1
             acc = [accp.tile([P, NB], F32, name="acc%d" % j, tag="acc") for j in range(NJ)]
             zq = keep.tile([P, H], F32, name="z_" + name)
             z[name] = zq
 
-            def mx_pass(ci, wt, j):
-                a, plane, k = chunks[ci][2], chunks[ci][3], chunks[ci][4]
+            def load_pair(s, cuts):
+                wt = wpool.tile([P, 2, H], U32, name="wt", tag="wt", align_bytes=64)
+                pair = wx if s == 0 else wh[2 * (s - 1):2 * s]
+                src = pair.rearrange("g p n t -> p g (n t)").bitcast(I32)
+                for e, js in cuts:
+                    nc.sync.dma_start(out=wt[:, e, js].bitcast(I32), in_=src[:, e, js])
+                return wt
+
+            def mx_pass(s, wt, e, j):
+                plane = xplanes[q // 2] if s == 0 else hplanes[q]
+                k = 8 * (q % 2) + 4 * e if s == 0 else 8 * (s - 1) + 4 * e
                 nc.tensor.matmul_mx(
                     out=acc[j][:],
-                    lhsT=a_codes[:, P * a:P * (a + 1)].bitcast(FP8X4),
-                    lhsT_scale=a_scales[:, P * a:P * (a + 1)],
-                    rhs=wt[:, cols[j]].bitcast(FP8X4),
+                    lhsT=a_codes[:, s, e, :].bitcast(FP8X4),
+                    lhsT_scale=a_scales[:, s, e, :],
+                    rhs=wt[:, e, cols[j]].bitcast(FP8X4),
                     rhs_scale=plane[k:P, cols[j]],
-                    start=(ci == 0),
-                    stop=(ci == last),
+                    start=(s == 0 and e == 0),
+                    stop=(s == PAIRS - 1 and e == 1),
                 )
 
             def gate_value(j):
@@ -172,22 +163,27 @@ def tile_simplelstm_w_kernel(
                     nc.vector.tensor_tensor(out=zq[:, js], in0=zq[:, js], in1=tanh_c[:, js], op=ALU.mult)
                     nc.sync.dma_start(out=out_0[:, js], in_=zq[:, js])
 
-            for ci in range(whole):
-                wt = wpool.tile([P, H], U32, name="wt", tag="wt", align_bytes=64)
-                load(wt, chunks[ci][0], chunks[ci][1], slice(0, H))
-                for j in range(NJ):
-                    mx_pass(ci, wt, j)
+            both = [(slice(0, 2), slice(0, H))]
+            by_group = [(slice(e, e + 1), slice(0, H)) for e in range(2)]
+            by_block = [(slice(e, e + 1), cols[j]) for j in range(NJ) for e in range(2)]
 
-            tapered = [wpool.tile([P, H], U32, name="wt", tag="wt", align_bytes=64) for ci in range(whole, len(chunks))]
-            for j in range(NJ):
-                for ci in range(whole, len(chunks)):
-                    load(tapered[ci - whole], chunks[ci][0], chunks[ci][1], cols[j])
-            if q == 3:
+            for s in range(PAIRS - 1):
+                wt = load_pair(s, by_group if (final_gate and s == 1) else both)
+                for e in range(2):
+                    for j in range(NJ):
+                        mx_pass(s, wt, e, j)
+                if s == 0:
+                    for j in range(NJ):
+                        pb = auxp.tile([P, NB], F32, name="pb", tag="aux")
+                        nc.tensor.matmul(out=pb[:], lhsT=sel[:, q, :], rhs=brow[:, cols[j]], start=True, stop=True)
+                        nc.scalar.copy(out=bias_bc[:, q, cols[j]], in_=pb[:])
+
+            wt = load_pair(PAIRS - 1, by_block if final_gate else both)
+            if final_gate:
                 nc.sync.dma_start(out=out_1, in_=c_t[:])
-
             for j in range(NJ):
-                for ci in range(whole, len(chunks)):
-                    mx_pass(ci, tapered[ci - whole], j)
+                for e in range(2):
+                    mx_pass(PAIRS - 1, wt, e, j)
                 gate_value(j)
                 if j > 0:
                     combine(j - 1)

@@ -74,14 +74,14 @@ def tile_simplelstm_w_kernel(
             sx, sh = gates[q][2], gates[q][4]
             lo = 8 * (q % 2)
             for quad in range(4):
-                nc.gpsimd.dma_start(
-                    out=xplanes[q // 2][32 * quad + lo:32 * quad + lo + 8, :].bitcast(F32),
-                    in_=sx[:, 4 * quad:4 * quad + 4, :].bitcast(F32),
+                nc.sync.dma_start(
+                    out=xplanes[q // 2][32 * quad + lo:32 * quad + lo + 8, :].bitcast(I32),
+                    in_=sx[:, 4 * quad:4 * quad + 4, :].bitcast(I32),
                 )
             for quad in range(4):
-                nc.gpsimd.dma_start(
-                    out=hplanes[q][32 * quad:32 * quad + 16, :].bitcast(F32),
-                    in_=sh[:, 4 * quad:4 * quad + 4, :].bitcast(F32),
+                nc.sync.dma_start(
+                    out=hplanes[q][32 * quad:32 * quad + 16, :].bitcast(I32),
+                    in_=sh[:, 4 * quad:4 * quad + 4, :].bitcast(I32),
                 )
 
         a_codes = keep.tile([P, PAIRS, 2, P], U32, name="a_codes", align_bytes=64)

@@ -74,9 +74,9 @@ def tile_simplelstm_w_kernel(
             sx, sh = gates[q][2], gates[q][4]
             lo = 8 * (q % 2)
             for quad in range(4):
-                nc.sync.dma_start(
-                    out=xplanes[q // 2][32 * quad + lo:32 * quad + lo + 8, :].bitcast(I32),
-                    in_=sx[:, 4 * quad:4 * quad + 4, :].bitcast(I32),
+                nc.gpsimd.dma_start(
+                    out=xplanes[q // 2][32 * quad + lo:32 * quad + lo + 8, :].bitcast(F32),
+                    in_=sx[:, 4 * quad:4 * quad + 4, :].bitcast(F32),
                 )
             for quad in range(4):
                 nc.sync.dma_start(

@@ -67,21 +67,25 @@ def tile_simplelstm_w_kernel(
         nc.vector.memset(sel[:], 0.0)
         for q in range(4):
             nc.vector.memset(sel[32 * q:32 * q + 1, q, :], 1.0)
-        for q in range(4):
-            nc.scalar.dma_start(out=brow[32 * q:32 * q + 1, :], in_=gates[q][5].rearrange("(o n) -> o n", o=1))
+
+        def load_h_scales(q, quad):
+            nc.sync.dma_start(
+                out=hplanes[q][32 * quad:32 * quad + 16, :].bitcast(I32),
+                in_=gates[q][4][:, 4 * quad:4 * quad + 4, :].bitcast(I32),
+            )
 
         for q in range(4):
-            sx, sh = gates[q][2], gates[q][4]
+            for quad in (2, 3):
+                load_h_scales(q, quad)
+        low_quads = [(q, quad) for q in range(4) for quad in (0, 1)]
+
+        for q in range(4):
+            sx = gates[q][2]
             lo = 8 * (q % 2)
             for quad in range(4):
                 nc.gpsimd.dma_start(
                     out=xplanes[q // 2][32 * quad + lo:32 * quad + lo + 8, :].bitcast(F32),
                     in_=sx[:, 4 * quad:4 * quad + 4, :].bitcast(F32),
-                )
-            for quad in range(4):
-                nc.sync.dma_start(
-                    out=hplanes[q][32 * quad:32 * quad + 16, :].bitcast(I32),
-                    in_=sh[:, 4 * quad:4 * quad + 4, :].bitcast(I32),
                 )
 
         a_codes = keep.tile([P, PAIRS, 2, P], U32, name="a_codes", align_bytes=64)
@@ -169,6 +173,12 @@ def tile_simplelstm_w_kernel(
 
             for s in range(PAIRS - 1):
                 wt = load_pair(s, by_group if (final_gate and s == 1) else both)
+                for q_low, quad in low_quads[:3]:
+                    load_h_scales(q_low, quad)
+                low_quads = low_quads[3:]
+                if q == 0 and s == 0:
+                    for b in range(4):
+                        nc.scalar.dma_start(out=brow[32 * b:32 * b + 1, :], in_=gates[b][5].rearrange("(o n) -> o n", o=1))
                 for e in range(2):
                     for j in range(NJ):
                         mx_pass(s, wt, e, j)

@@ -78,15 +78,18 @@ def tile_simplelstm_w_kernel(
             for quad in (2, 3):
                 load_h_scales(q, quad)
         low_quads = [(q, quad) for q in range(4) for quad in (0, 1)]
+        for q, quad in low_quads[:3]:
+            load_h_scales(q, quad)
+        low_quads = low_quads[3:]
 
-        for q in range(4):
-            sx = gates[q][2]
-            lo = 8 * (q % 2)
+        for pair in range(2):
             for quad in range(4):
-                nc.gpsimd.dma_start(
-                    out=xplanes[q // 2][32 * quad + lo:32 * quad + lo + 8, :].bitcast(F32),
-                    in_=sx[:, 4 * quad:4 * quad + 4, :].bitcast(F32),
-                )
+                for q in (2 * pair, 2 * pair + 1):
+                    lo = 8 * (q % 2)
+                    nc.gpsimd.dma_start(
+                        out=xplanes[pair][32 * quad + lo:32 * quad + lo + 8, :].bitcast(F32),
+                        in_=gates[q][2][:, 4 * quad:4 * quad + 4, :].bitcast(F32),
+                    )
 
         a_codes = keep.tile([P, PAIRS, 2, P], U32, name="a_codes", align_bytes=64)
         a_scales = keep.tile([P, PAIRS, 2, P], U8, name="a_scales", align_bytes=64)

@@ -44,20 +44,20 @@ def tile_simplelstm_w_kernel(
         wpool = ctx.enter_context(tc.tile_pool(name="weights", bufs=W_BUFS))
         accp = ctx.enter_context(tc.psum_pool(name="acc", bufs=6))
         auxp = ctx.enter_context(tc.psum_pool(name="aux", bufs=2))
+        ctx.enter_context(tc.manual_schedule(engines={mybir.EngineType.SP}))
 
         x_sb = keep.tile([P, IN], BF16, name="x_sb")
         nc.sync.dma_start(out=x_sb[:], in_=x)
         h_sb = keep.tile([P, H], BF16, name="h_sb")
         nc.sync.dma_start(out=h_sb[:], in_=h0)
         c_sb = keep.tile([P, H], BF16, name="c_sb")
-        nc.sync.dma_start(out=c_sb[:], in_=c0)
 
         xplanes = [keep.tile([P, H], U8, name="xplane%d" % s, align_bytes=64) for s in range(2)]
         hplanes = [keep.tile([P, H], U8, name="hplane%d" % q, align_bytes=64) for q in range(4)]
         for q in range(4):
+            nc.vector.memset(hplanes[q][:].bitcast(I32), 0)
             if q % 2 == 0:
                 nc.vector.memset(xplanes[q // 2][:].bitcast(I32), 0)
-            nc.vector.memset(hplanes[q][:].bitcast(I32), 0)
 
         ident = keep.tile([P, P], F32, name="ident")
         make_identity(nc, ident[:])
@@ -68,28 +68,38 @@ def tile_simplelstm_w_kernel(
         for q in range(4):
             nc.vector.memset(sel[32 * q:32 * q + 1, q, :], 1.0)
 
-        def load_h_scales(q, quad):
-            nc.sync.dma_start(
-                out=hplanes[q][32 * quad:32 * quad + 16, :].bitcast(I32),
-                in_=gates[q][4][:, 4 * quad:4 * quad + 4, :].bitcast(I32),
+        def load_h_scales(engine, dtype, q, quad):
+            engine.dma_start(
+                out=hplanes[q][32 * quad:32 * quad + 16, :].bitcast(dtype),
+                in_=gates[q][4][:, 4 * quad:4 * quad + 4, :].bitcast(dtype),
             )
 
-        for q in range(4):
-            for quad in (2, 3):
-                load_h_scales(q, quad)
+        def load_x_scales(pair, quad):
+            for q in (2 * pair, 2 * pair + 1):
+                lo = 8 * (q % 2)
+                nc.gpsimd.dma_start(
+                    out=xplanes[pair][32 * quad + lo:32 * quad + lo + 8, :].bitcast(F32),
+                    in_=gates[q][2][:, 4 * quad:4 * quad + 4, :].bitcast(F32),
+                )
+
         low_quads = [(q, quad) for q in range(4) for quad in (0, 1)]
-        for q, quad in low_quads[:3]:
-            load_h_scales(q, quad)
-        low_quads = low_quads[3:]
+
+        def load_low_quads(count):
+            for q, quad in low_quads[:count]:
+                load_h_scales(nc.sync, I32, q, quad)
+                low_quads.remove((q, quad))
+
+        load_low_quads(2)
 
         for pair in range(2):
-            for quad in range(4):
-                for q in (2 * pair, 2 * pair + 1):
-                    lo = 8 * (q % 2)
-                    nc.gpsimd.dma_start(
-                        out=xplanes[pair][32 * quad + lo:32 * quad + lo + 8, :].bitcast(F32),
-                        in_=gates[q][2][:, 4 * quad:4 * quad + 4, :].bitcast(F32),
-                    )
+            load_x_scales(pair, 0)
+            load_x_scales(pair, 2)
+            load_x_scales(pair, 3)
+            load_h_scales(nc.gpsimd, F32, 2 * pair, 2)
+            load_x_scales(pair, 1)
+            load_h_scales(nc.gpsimd, F32, 2 * pair, 3)
+            load_h_scales(nc.gpsimd, F32, 2 * pair + 1, 2)
+            load_h_scales(nc.gpsimd, F32, 2 * pair + 1, 3)
 
         a_codes = keep.tile([P, PAIRS, 2, P], U32, name="a_codes", align_bytes=64)
         a_scales = keep.tile([P, PAIRS, 2, P], U8, name="a_scales", align_bytes=64)
@@ -176,10 +186,9 @@ def tile_simplelstm_w_kernel(
 
             for s in range(PAIRS - 1):
                 wt = load_pair(s, by_group if (final_gate and s == 1) else both)
-                for q_low, quad in low_quads[:3]:
-                    load_h_scales(q_low, quad)
-                low_quads = low_quads[3:]
+                load_low_quads(2)
                 if q == 0 and s == 0:
+                    nc.sync.dma_start(out=c_sb[:], in_=c0)
                     for b in range(4):
                         nc.scalar.dma_start(out=brow[32 * b:32 * b + 1, :], in_=gates[b][5].rearrange("(o n) -> o n", o=1))
                 for e in range(2):

from contextlib import ExitStack

import concourse.mybir as mybir
from concourse.masks import make_identity

F32 = mybir.dt.float32
BF16 = mybir.dt.bfloat16
I32 = mybir.dt.int32
U32 = mybir.dt.uint32
U8 = mybir.dt.uint8
FP8X4 = mybir.dt.float8_e4m3fn_x4
ACT = mybir.ActivationFunctionType
ALU = mybir.AluOpType

P = 128
B, IN, H = 128, 1024, 2048
NB = 512
NJ = H // NB
PAIRS = 3
FLOPS = 2 * B * (IN + H) * 4 * H

W_BUFS = 7


def tile_simplelstm_w_kernel(
    tc, x, h0, c0,
    W_xi_words, W_xi_scales, W_xf_words, W_xf_scales,
    W_xo_words, W_xo_scales, W_xc_words, W_xc_scales,
    b_xi, b_xf, b_xo, b_xc,
    W_hi_words, W_hi_scales, W_hf_words, W_hf_scales,
    W_ho_words, W_ho_scales, W_hc_words, W_hc_scales,
    out_0, out_1,
):
    nc = tc.nc
    gates = (
        ("i", W_xi_words, W_xi_scales, W_hi_words, W_hi_scales, b_xi, ACT.Sigmoid),
        ("c", W_xc_words, W_xc_scales, W_hc_words, W_hc_scales, b_xc, ACT.Tanh),
        ("f", W_xf_words, W_xf_scales, W_hf_words, W_hf_scales, b_xf, ACT.Sigmoid),
        ("o", W_xo_words, W_xo_scales, W_ho_words, W_ho_scales, b_xo, ACT.Sigmoid),
    )
    cols = [slice(NB * j, NB * (j + 1)) for j in range(NJ)]
    with ExitStack() as ctx:
        keep = ctx.enter_context(tc.tile_pool(name="keep", bufs=1))
        wpool = ctx.enter_context(tc.tile_pool(name="weights", bufs=W_BUFS))
        accp = ctx.enter_context(tc.psum_pool(name="acc", bufs=6))
        auxp = ctx.enter_context(tc.psum_pool(name="aux", bufs=2))
        ctx.enter_context(tc.manual_schedule(engines={mybir.EngineType.SP}))

        x_sb = keep.tile([P, IN], BF16, name="x_sb")
        nc.sync.dma_start(out=x_sb[:], in_=x)
        h_sb = keep.tile([P, H], BF16, name="h_sb")
        nc.sync.dma_start(out=h_sb[:], in_=h0)
        c_sb = keep.tile([P, H], BF16, name="c_sb")

        xplanes = [keep.tile([P, H], U8, name="xplane%d" % s, align_bytes=64) for s in range(2)]
        hplanes = [keep.tile([P, H], U8, name="hplane%d" % q, align_bytes=64) for q in range(4)]
        for q in range(4):
            nc.vector.memset(hplanes[q][:].bitcast(I32), 0)
            if q % 2 == 0:
                nc.vector.memset(xplanes[q // 2][:].bitcast(I32), 0)

        ident = keep.tile([P, P], F32, name="ident")
        make_identity(nc, ident[:])
        brow = keep.tile([P, H], BF16, name="brow")
        nc.vector.memset(brow[:].bitcast(I32), 0)
        sel = keep.tile([P, 4, P], BF16, name="sel")
        nc.vector.memset(sel[:], 0.0)
        for q in range(4):
            nc.vector.memset(sel[32 * q:32 * q + 1, q, :], 1.0)

        def load_h_scales(engine, dtype, q, quad):
            engine.dma_start(
                out=hplanes[q][32 * quad:32 * quad + 16, :].bitcast(dtype),
                in_=gates[q][4][:, 4 * quad:4 * quad + 4, :].bitcast(dtype),
            )

        def load_x_scales(pair, quad):
            for q in (2 * pair, 2 * pair + 1):
                lo = 8 * (q % 2)
                nc.gpsimd.dma_start(
                    out=xplanes[pair][32 * quad + lo:32 * quad + lo + 8, :].bitcast(F32),
                    in_=gates[q][2][:, 4 * quad:4 * quad + 4, :].bitcast(F32),
                )

        low_quads = [(q, quad) for q in range(4) for quad in (0, 1)]

        def load_low_quads(count):
            for q, quad in low_quads[:count]:
                load_h_scales(nc.sync, I32, q, quad)
                low_quads.remove((q, quad))

        load_low_quads(2)

        for pair in range(2):
            load_x_scales(pair, 0)
            load_x_scales(pair, 2)
            load_x_scales(pair, 3)
            load_h_scales(nc.gpsimd, F32, 2 * pair, 2)
            load_x_scales(pair, 1)
            load_h_scales(nc.gpsimd, F32, 2 * pair, 3)
            load_h_scales(nc.gpsimd, F32, 2 * pair + 1, 2)
            load_h_scales(nc.gpsimd, F32, 2 * pair + 1, 3)

        a_codes = keep.tile([P, PAIRS, 2, P], U32, name="a_codes", align_bytes=64)
        a_scales = keep.tile([P, PAIRS, 2, P], U8, name="a_scales", align_bytes=64)
        sources = (
            x_sb[:].bitcast(F32),
            h_sb[:].bitcast(F32)[:, 0:512],
            h_sb[:].bitcast(F32)[:, 512:1024],
        )
        grouped = []
        for s, words in enumerate(sources):
            bank = auxp.tile([P, 4, P], F32, name="tp", tag="aux")
            for g in range(2):
                for u in range(2):
                    nc.tensor.transpose(
                        bank[:, 2 * g + u, :],
                        words[:, 256 * g + u:256 * (g + 1):2],
                        ident[:],
                    )
            grp = keep.tile([P, 1024], BF16, name="grouped%d" % s, align_bytes=64)
            nc.vector.tensor_copy(
                out=grp[:].bitcast(F32).rearrange("p (g m u) -> p g m u", g=2, u=2),
                in_=bank[:].rearrange("p (g u) m -> p g m u", u=2),
            )
            grouped.append(grp)
        for s in range(PAIRS):
            nc.vector.quantize_mx(
                out=a_codes[:, s, :, :].rearrange("p g m -> p (g m)").bitcast(FP8X4),
                scales=a_scales[:, s, :, :].rearrange("p g m -> p (g m)"),
                in_=grouped[s][:],
            )

        bias_bc = keep.tile([P, 4, H], BF16, name="bias_bc")
        z = {}
        c_t = keep.tile([P, H], F32, name="c_t")
        tanh_c = keep.tile([P, H], F32, name="tanh_c")

        for q, (name, wx, sx, wh, sh, bias, func) in enumerate(gates):
            final_gate = q == len(gates) - 1
            acc = [accp.tile([P, NB], F32, name="acc%d" % j, tag="acc") for j in range(NJ)]
            zq = keep.tile([P, H], F32, name="z_" + name)
            z[name] = zq

            def load_pair(s, cuts):
                wt = wpool.tile([P, 2, H], U32, name="wt", tag="wt", align_bytes=64)
                pair = wx if s == 0 else wh[2 * (s - 1):2 * s]
                src = pair.rearrange("g p n t -> p g (n t)").bitcast(I32)
                for e, js in cuts:
                    nc.sync.dma_start(out=wt[:, e, js].bitcast(I32), in_=src[:, e, js])
                return wt

            def mx_pass(s, wt, e, j):
                plane = xplanes[q // 2] if s == 0 else hplanes[q]
                k = 8 * (q % 2) + 4 * e if s == 0 else 8 * (s - 1) + 4 * e
                nc.tensor.matmul_mx(
                    out=acc[j][:],
                    lhsT=a_codes[:, s, e, :].bitcast(FP8X4),
                    lhsT_scale=a_scales[:, s, e, :],
                    rhs=wt[:, e, cols[j]].bitcast(FP8X4),
                    rhs_scale=plane[k:P, cols[j]],
                    start=(s == 0 and e == 0),
                    stop=(s == PAIRS - 1 and e == 1),
                )

            def gate_value(j):
                js = cols[j]
                nc.vector.tensor_tensor(out=zq[:, js], in0=acc[j][:], in1=bias_bc[:, q, js], op=ALU.add)
                nc.scalar.activation(out=zq[:, js], in_=zq[:, js], func=func)

            def combine(j):
                js = cols[j]
                if name == "c":
                    nc.vector.tensor_tensor(out=zq[:, js], in0=zq[:, js], in1=z["i"][:, js], op=ALU.mult)
                if name == "f":
                    nc.vector.tensor_tensor(out=zq[:, js], in0=zq[:, js], in1=c_sb[:, js], op=ALU.mult)
                    nc.vector.tensor_tensor(out=c_t[:, js], in0=zq[:, js], in1=z["c"][:, js], op=ALU.add)
                    nc.scalar.activation(out=tanh_c[:, js], in_=c_t[:, js], func=ACT.Tanh)
                if name == "o":
                    nc.vector.tensor_tensor(out=zq[:, js], in0=zq[:, js], in1=tanh_c[:, js], op=ALU.mult)
                    nc.sync.dma_start(out=out_0[:, js], in_=zq[:, js])

            both = [(slice(0, 2), slice(0, H))]
            by_group = [(slice(e, e + 1), slice(0, H)) for e in range(2)]
            by_block = [(slice(e, e + 1), cols[j]) for j in range(NJ) for e in range(2)]

            for s in range(PAIRS - 1):
                wt = load_pair(s, by_group if (final_gate and s == 1) else both)
                load_low_quads(2)
                if q == 0 and s == 0:
                    nc.sync.dma_start(out=c_sb[:], in_=c0)
                    for b in range(4):
                        nc.scalar.dma_start(out=brow[32 * b:32 * b + 1, :], in_=gates[b][5].rearrange("(o n) -> o n", o=1))
                for e in range(2):
                    for j in range(NJ):
                        mx_pass(s, wt, e, j)
                if s == 0:
                    for j in range(NJ):
                        pb = auxp.tile([P, NB], F32, name="pb", tag="aux")
                        nc.tensor.matmul(out=pb[:], lhsT=sel[:, q, :], rhs=brow[:, cols[j]], start=True, stop=True)
                        nc.scalar.copy(out=bias_bc[:, q, cols[j]], in_=pb[:])

            wt = load_pair(PAIRS - 1, by_block if final_gate else both)
            if final_gate:
                nc.sync.dma_start(out=out_1, in_=c_t[:])
            for j in range(NJ):
                for e in range(2):
                    mx_pass(PAIRS - 1, wt, e, j)
                gate_value(j)
                if j > 0:
                    combine(j - 1)
            combine(NJ - 1)
